import numpy as np
import ml_dtypes


def mxq(x, axis, fmt="e4m3"):
    dtype, down = {"e4m3": (ml_dtypes.float8_e4m3fn, 7), "e5m2": (ml_dtypes.float8_e5m2, 14)}[fmt]
    v = np.moveaxis(np.asarray(x, np.float32).astype(ml_dtypes.bfloat16).astype(np.float64), axis, -1)
    blocks = v.reshape(v.shape[:-1] + (-1, 32))
    amax = np.abs(blocks).max(-1, keepdims=True)
    byte = np.maximum(np.where(amax > 0, np.frexp(amax)[1] - 1 + 127, 0) - down, 1)
    scale = np.exp2(byte - 127.0)
    codes = (blocks / scale).astype(np.float32).astype(dtype).astype(np.float64)
    return np.moveaxis((codes * scale).reshape(v.shape), -1, axis)


WIDE = False


def mx_kscale(k):
    if not WIDE:
        return np.ones(k)
    levels = np.array([10, -10, 5, -5, 0])
    a = np.random.permutation(np.resize(levels, k // 512 * 4)).reshape(k // 512, 4)
    idx = np.arange(k)
    return np.exp2(a[idx // 512, idx % 128 // 32])


BF16 = ml_dtypes.bfloat16


def bf(x):
    return np.asarray(x, np.float32).astype(BF16)


def f64(x):
    return np.asarray(x).astype(np.float64)


B, T, C, NH, HS, NLQ, NLKV, DHR = 4, 1024, 512, 4, 128, 512, 512, 128


def setup_inputs():
    s, t = mx_kscale(C), mx_kscale(NLKV)
    return {"y_lat": bf(np.random.standard_normal((B, NH, T, NLKV)) * 0.35 / t),
            "W_uv": bf(np.random.standard_normal((C, NLKV)) * 2.0 / np.sqrt(NLKV) * s[:, None] * t[None, :]),
            "W_o": bf(np.random.standard_normal((C, C)) / np.sqrt(C) / s[None, :])}


def reference(y_lat, W_uv, W_o):
    v_flat = mxq(f64(W_uv), 0, "e4m3").T @ mxq(f64(W_o), 1, "e4m3").T
    v_eff = v_flat.reshape(NLKV, NH, HS).transpose(1, 0, 2)
    y = mxq(f64(y_lat), 3, "e4m3") @ mxq(v_eff, 1, "e4m3")[None]
    return y.transpose(0, 2, 1, 3).reshape(B, T, C)

@@ -1,0 +1,158 @@
+from contextlib import ExitStack
+
+import concourse.mybir as mybir
+from concourse.masks import make_identity
+
+BF16 = mybir.dt.bfloat16
+F32 = mybir.dt.float32
+U32 = mybir.dt.uint32
+U8 = mybir.dt.uint8
+FP8X4 = mybir.dt.float8_e4m3fn_x4
+
+P = 128
+PACK = 4
+K = P * PACK
+WORDS = K // 2
+HALVES = WORDS // P
+
+B, NH, T, HS = 4, 4, 1024, 128
+C = NH * HS
+ROW_TILES = T // P
+PAIR = 2
+GROUPS_PER_BANK = 4
+
+Y_TILES_IN_SBUF = 12
+
+FLOPS = 2 * K * K * C + 2 * B * NH * T * K * HS
+
+
+def quantise_last_axis(nc, pools, identity, rows, row_tiles, codes, scales):
+    row_words = rows.bitcast(F32)
+    grouped = pools["grouped"].tile([P, row_tiles * P * PACK], BF16, tag="grouped", align_bytes=64)
+    grouped_words = grouped[:].bitcast(F32)
+    bank_words = PAIR * P * HALVES
+    for pair in range(row_tiles // PAIR):
+        planes = pools["planes"].tile([P, HALVES, PAIR * P], F32, tag="planes")
+        for i in range(PAIR):
+            for u in range(HALVES):
+                first = (pair * PAIR + i) * WORDS + u * P
+                nc.tensor.transpose(
+                    planes[:, u, i * P : (i + 1) * P], row_words[:, first : first + P], identity
+                )
+        nc.scalar.copy(
+            out=grouped_words[:, pair * bank_words : (pair + 1) * bank_words].rearrange(
+                "p (n u) -> p n u", u=HALVES
+            ),
+            in_=planes[:].rearrange("p u n -> p n u"),
+        )
+    nc.vector.quantize_mx(out=codes.bitcast(FP8X4), scales=scales, in_=grouped[:])
+
+
+def tile_causalselfattention_pc_t_kernel(tc, y_lat, W_uv, W_o, out):
+    nc = tc.nc
+    with ExitStack() as ctx:
+        keep = ctx.enter_context(tc.tile_pool(name="keep", bufs=1))
+        y_pool = ctx.enter_context(tc.tile_pool(name="y_rows", bufs=Y_TILES_IN_SBUF))
+        out_pool = ctx.enter_context(tc.tile_pool(name="result", bufs=B))
+        mx_pool = ctx.enter_context(tc.tile_pool(name="mx", bufs=3))
+        pools = {
+            "grouped": ctx.enter_context(tc.tile_pool(name="grouped", bufs=3)),
+            "planes": ctx.enter_context(tc.psum_pool(name="planes", bufs=4)),
+        }
+        acc_pool = ctx.enter_context(tc.psum_pool(name="acc", bufs=4))
+
+        identity = keep.tile([P, P], F32)
+        make_identity(nc, identity[:])
+
+        wo_rows = keep.tile([P, NH * K], BF16)
+        nc.sync.dma_start(
+            out=wo_rows[:].rearrange("p (h j) -> p h j", h=NH),
+            in_=W_o.rearrange("(h p) j -> p h j", p=P),
+        )
+        uv_rows = keep.tile([P, PACK, K], BF16)
+        nc.sync.dma_start(
+            out=uv_rows[:].rearrange("p (u e) l -> p u e l", u=HALVES),
+            in_=W_uv.rearrange("(u p e) l -> p u e l", u=HALVES, p=P),
+        )
+
+        y_order = [(b, h) for b in range(B) for h in range(NH)]
+        y_rows = {}
+
+        def load_y(n):
+            b, h = y_order[n]
+            y_rows[n] = y_pool.tile([P, ROW_TILES * K], BF16, name="y_rows")
+            nc.sync.dma_start(
+                out=y_rows[n][:], in_=y_lat[b, h].rearrange("(p i) l -> p (i l)", i=ROW_TILES)
+            )
+
+        for n in range(Y_TILES_IN_SBUF):
+            load_y(n)
+
+        wo_codes = keep.tile([P, C], U32, align_bytes=64)
+        wo_scales = keep.tile([P, C], U8, align_bytes=64)
+        quantise_last_axis(nc, pools, identity[:], wo_rows[:], NH, wo_codes[:], wo_scales[:])
+
+        uv_grouped = pools["grouped"].tile([P, K * PACK], BF16, tag="grouped", align_bytes=64)
+        uv_by_code = uv_rows[:].rearrange("p t (u m e) -> p t u m e", u=HALVES, m=P)
+        for u in range(HALVES):
+            for e in range(2):
+                code = 2 * u + e
+                nc.vector.tensor_copy(
+                    out=uv_grouped[:, code * K : (code + 1) * K].rearrange("p (m t) -> p m t", t=PACK),
+                    in_=uv_by_code[:, :, u, :, e].rearrange("p t m -> p m t"),
+                )
+        uv_codes = keep.tile([P, K], U32, align_bytes=64)
+        uv_scales = keep.tile([P, K], U8, align_bytes=64)
+        nc.vector.quantize_mx(out=uv_codes[:].bitcast(FP8X4), scales=uv_scales[:], in_=uv_grouped[:])
+
+        v_grouped = pools["grouped"].tile([P, C * PACK], BF16, tag="grouped", align_bytes=64)
+        for h in range(NH):
+            head = slice(h * HS, (h + 1) * HS)
+            v_acc = acc_pool.tile([P, PACK, HS], F32, tag="acc")
+            for code in range(PACK):
+                latent = slice(code * P, (code + 1) * P)
+                nc.tensor.matmul_mx(
+                    out=v_acc[:, code, :],
+                    lhsT=uv_codes[:, latent].bitcast(FP8X4),
+                    lhsT_scale=uv_scales[:, latent],
+                    rhs=wo_codes[:, head].bitcast(FP8X4),
+                    rhs_scale=wo_scales[:, head],
+                    start=True,
+                    stop=True,
+                )
+            nc.vector.tensor_copy(
+                out=v_grouped[:, h * HS * PACK : (h + 1) * HS * PACK].rearrange("p (s t) -> p s t", t=PACK),
+                in_=v_acc[:].rearrange("p t s -> p s t"),
+            )
+        v_codes = keep.tile([P, C], U32, align_bytes=64)
+        v_scales = keep.tile([P, C], U8, align_bytes=64)
+        nc.vector.quantize_mx(out=v_codes[:].bitcast(FP8X4), scales=v_scales[:], in_=v_grouped[:])
+
+        for b in range(B):
+            result = out_pool.tile([P, ROW_TILES, C], F32)
+            for h in range(NH):
+                n = b * NH + h
+                if n + Y_TILES_IN_SBUF < len(y_order):
+                    load_y(n + Y_TILES_IN_SBUF)
+                head = slice(h * HS, (h + 1) * HS)
+                y_codes = mx_pool.tile([P, ROW_TILES * P], U32, align_bytes=64)
+                y_scales = mx_pool.tile([P, ROW_TILES * P], U8, align_bytes=64)
+                quantise_last_axis(nc, pools, identity[:], y_rows[n][:], ROW_TILES, y_codes[:], y_scales[:])
+                for first in range(0, ROW_TILES, GROUPS_PER_BANK):
+                    acc = acc_pool.tile([P, GROUPS_PER_BANK, HS], F32, tag="acc")
+                    for g in range(GROUPS_PER_BANK):
+                        tokens = slice((first + g) * P, (first + g + 1) * P)
+                        nc.tensor.matmul_mx(
+                            out=acc[:, g, :],
+                            lhsT=y_codes[:, tokens].bitcast(FP8X4),
+                            lhsT_scale=y_scales[:, tokens],
+                            rhs=v_codes[:, head].bitcast(FP8X4),
+                            rhs_scale=v_scales[:, head],
+                            start=True,
+                            stop=True,
+                        )
+                    nc.vector.tensor_copy(out=result[:, first : first + GROUPS_PER_BANK, head], in_=acc[:])
+            nc.sync.dma_start(
+                out=out[b].rearrange("(p i) c -> p (i c)", i=ROW_TILES),
+                in_=result[:].rearrange("p i c -> p (i c)"),
+            )

@@ -17,16 +17,18 @@ HALVES = WORDS // P
 
 B, NH, T, HS = 4, 4, 1024, 128
 C = NH * HS
+Y_TILES = B * NH
 ROW_TILES = T // P
 PAIR = 2
 GROUPS_PER_BANK = 4
 
 Y_TILES_IN_SBUF = 12
+MULTIPLY_LAG = 2
 
 FLOPS = 2 * K * K * C + 2 * B * NH * T * K * HS
 
 
-def quantise_last_axis(nc, pools, identity, rows, row_tiles, codes, scales):
+def transpose_rows(nc, pools, identity, rows, row_tiles):
     row_words = rows.bitcast(F32)
     grouped = pools["grouped"].tile([P, row_tiles * P * PACK], BF16, tag="grouped", align_bytes=64)
     grouped_words = grouped[:].bitcast(F32)
@@ -35,9 +37,9 @@ def quantise_last_axis(nc, pools, identity, rows, row_tiles, codes, scales):
         planes = pools["planes"].tile([P, HALVES, PAIR * P], F32, tag="planes")
         for i in range(PAIR):
             for u in range(HALVES):
-                first = (pair * PAIR + i) * WORDS + u * P
+                word = (pair * PAIR + i) * WORDS + u * P
                 nc.tensor.transpose(
-                    planes[:, u, i * P : (i + 1) * P], row_words[:, first : first + P], identity
+                    planes[:, u, i * P : (i + 1) * P], row_words[:, word : word + P], identity
                 )
         nc.scalar.copy(
             out=grouped_words[:, pair * bank_words : (pair + 1) * bank_words].rearrange(
@@ -45,7 +47,11 @@ def quantise_last_axis(nc, pools, identity, rows, row_tiles, codes, scales):
             ),
             in_=planes[:].rearrange("p u n -> p n u"),
         )
-    nc.vector.quantize_mx(out=codes.bitcast(FP8X4), scales=scales, in_=grouped[:])
+    return grouped
+
+
+def quantise(nc, grouped, codes, scales):
+    nc.vector.quantize_mx(out=codes[:].bitcast(FP8X4), scales=scales[:], in_=grouped[:])
 
 
 def tile_causalselfattention_pc_t_kernel(tc, y_lat, W_uv, W_o, out):
@@ -60,37 +66,35 @@ def tile_causalselfattention_pc_t_kernel(tc, y_lat, W_uv, W_o, out):
             "planes": ctx.enter_context(tc.psum_pool(name="planes", bufs=4)),
         }
         acc_pool = ctx.enter_context(tc.psum_pool(name="acc", bufs=4))
+        ctx.enter_context(tc.manual_schedule())
 
         identity = keep.tile([P, P], F32)
         make_identity(nc, identity[:])
 
-        wo_rows = keep.tile([P, NH * K], BF16)
-        nc.sync.dma_start(
-            out=wo_rows[:].rearrange("p (h j) -> p h j", h=NH),
-            in_=W_o.rearrange("(h p) j -> p h j", p=P),
-        )
         uv_rows = keep.tile([P, PACK, K], BF16)
         nc.sync.dma_start(
             out=uv_rows[:].rearrange("p (u e) l -> p u e l", u=HALVES),
             in_=W_uv.rearrange("(u p e) l -> p u e l", u=HALVES, p=P),
         )
+        wo_rows = keep.tile([P, NH * K], BF16)
+        nc.sync.dma_start(
+            out=wo_rows[:].rearrange("p (h j) -> p h j", h=NH),
+            in_=W_o.rearrange("(h p) j -> p h j", p=P),
+        )
 
-        y_order = [(b, h) for b in range(B) for h in range(NH)]
         y_rows = {}
 
         def load_y(n):
-            b, h = y_order[n]
             y_rows[n] = y_pool.tile([P, ROW_TILES * K], BF16, name="y_rows")
             nc.sync.dma_start(
-                out=y_rows[n][:], in_=y_lat[b, h].rearrange("(p i) l -> p (i l)", i=ROW_TILES)
+                out=y_rows[n][:],
+                in_=y_lat[n // NH, n % NH].rearrange("(p i) l -> p (i l)", i=ROW_TILES),
             )
 
         for n in range(Y_TILES_IN_SBUF):
             load_y(n)
 
-        wo_codes = keep.tile([P, C], U32, align_bytes=64)
-        wo_scales = keep.tile([P, C], U8, align_bytes=64)
-        quantise_last_axis(nc, pools, identity[:], wo_rows[:], NH, wo_codes[:], wo_scales[:])
+        wo_grouped = transpose_rows(nc, pools, identity[:], wo_rows[:], NH)
 
         uv_grouped = pools["grouped"].tile([P, K * PACK], BF16, tag="grouped", align_bytes=64)
         uv_by_code = uv_rows[:].rearrange("p t (u m e) -> p t u m e", u=HALVES, m=P)
@@ -103,7 +107,53 @@ def tile_causalselfattention_pc_t_kernel(tc, y_lat, W_uv, W_o, out):
                 )
         uv_codes = keep.tile([P, K], U32, align_bytes=64)
         uv_scales = keep.tile([P, K], U8, align_bytes=64)
-        nc.vector.quantize_mx(out=uv_codes[:].bitcast(FP8X4), scales=uv_scales[:], in_=uv_grouped[:])
+        quantise(nc, uv_grouped, uv_codes, uv_scales)
+        wo_codes = keep.tile([P, C], U32, align_bytes=64)
+        wo_scales = keep.tile([P, C], U8, align_bytes=64)
+        quantise(nc, wo_grouped, wo_codes, wo_scales)
+
+        y_grouped, y_codes, y_scales, y_acc, results = {}, {}, {}, {}, {}
+        v_codes = keep.tile([P, C], U32, align_bytes=64)
+        v_scales = keep.tile([P, C], U8, align_bytes=64)
+
+        def transpose_y(n):
+            y_grouped[n] = transpose_rows(nc, pools, identity[:], y_rows[n][:], ROW_TILES)
+
+        def quantise_y(n):
+            y_codes[n] = mx_pool.tile([P, ROW_TILES * P], U32, name="y_codes", align_bytes=64)
+            y_scales[n] = mx_pool.tile([P, ROW_TILES * P], U8, name="y_scales", align_bytes=64)
+            quantise(nc, y_grouped[n], y_codes[n], y_scales[n])
+
+        def multiply_y(n):
+            head = slice((n % NH) * HS, (n % NH + 1) * HS)
+            y_acc[n] = []
+            for first in range(0, ROW_TILES, GROUPS_PER_BANK):
+                acc = acc_pool.tile([P, GROUPS_PER_BANK, HS], F32, tag="acc")
+                for g in range(GROUPS_PER_BANK):
+                    tokens = slice((first + g) * P, (first + g + 1) * P)
+                    nc.tensor.matmul_mx(
+                        out=acc[:, g, :],
+                        lhsT=y_codes[n][:, tokens].bitcast(FP8X4),
+                        lhsT_scale=y_scales[n][:, tokens],
+                        rhs=v_codes[:, head].bitcast(FP8X4),
+                        rhs_scale=v_scales[:, head],
+                        start=True,
+                        stop=True,
+                    )
+                y_acc[n].append(acc)
+
+        def empty_y(n):
+            b, h = n // NH, n % NH
+            if h == 0:
+                results[b] = out_pool.tile([P, ROW_TILES, C], F32, name="result")
+            out_rows = out[b].rearrange("(p i) c -> p i c", i=ROW_TILES)
+            for bank, acc in enumerate(y_acc[n]):
+                done = slice(bank * GROUPS_PER_BANK, (bank + 1) * GROUPS_PER_BANK)
+                nc.vector.tensor_copy(out=results[b][:, done, h * HS : (h + 1) * HS], in_=acc[:])
+                if h == NH - 1:
+                    nc.sync.dma_start(out=out_rows[:, done, :], in_=results[b][:, done, :])
+
+        transpose_y(0)
 
         v_grouped = pools["grouped"].tile([P, C * PACK], BF16, tag="grouped", align_bytes=64)
         for h in range(NH):
@@ -124,35 +174,16 @@ def tile_causalselfattention_pc_t_kernel(tc, y_lat, W_uv, W_o, out):
                 out=v_grouped[:, h * HS * PACK : (h + 1) * HS * PACK].rearrange("p (s t) -> p s t", t=PACK),
                 in_=v_acc[:].rearrange("p t s -> p s t"),
             )
-        v_codes = keep.tile([P, C], U32, align_bytes=64)
-        v_scales = keep.tile([P, C], U8, align_bytes=64)
-        nc.vector.quantize_mx(out=v_codes[:].bitcast(FP8X4), scales=v_scales[:], in_=v_grouped[:])
+        quantise(nc, v_grouped, v_codes, v_scales)
 
-        for b in range(B):
-            result = out_pool.tile([P, ROW_TILES, C], F32)
-            for h in range(NH):
-                n = b * NH + h
-                if n + Y_TILES_IN_SBUF < len(y_order):
-                    load_y(n + Y_TILES_IN_SBUF)
-                head = slice(h * HS, (h + 1) * HS)
-                y_codes = mx_pool.tile([P, ROW_TILES * P], U32, align_bytes=64)
-                y_scales = mx_pool.tile([P, ROW_TILES * P], U8, align_bytes=64)
-                quantise_last_axis(nc, pools, identity[:], y_rows[n][:], ROW_TILES, y_codes[:], y_scales[:])
-                for first in range(0, ROW_TILES, GROUPS_PER_BANK):
-                    acc = acc_pool.tile([P, GROUPS_PER_BANK, HS], F32, tag="acc")
-                    for g in range(GROUPS_PER_BANK):
-                        tokens = slice((first + g) * P, (first + g + 1) * P)
-                        nc.tensor.matmul_mx(
-                            out=acc[:, g, :],
-                            lhsT=y_codes[:, tokens].bitcast(FP8X4),
-                            lhsT_scale=y_scales[:, tokens],
-                            rhs=v_codes[:, head].bitcast(FP8X4),
-                            rhs_scale=v_scales[:, head],
-                            start=True,
-                            stop=True,
-                        )
-                    nc.vector.tensor_copy(out=result[:, first : first + GROUPS_PER_BANK, head], in_=acc[:])
-            nc.sync.dma_start(
-                out=out[b].rearrange("(p i) c -> p (i c)", i=ROW_TILES),
-                in_=result[:].rearrange("p i c -> p (i c)"),
-            )
+        for step in range(1, Y_TILES + MULTIPLY_LAG):
+            if step + Y_TILES_IN_SBUF - 1 < Y_TILES:
+                load_y(step + Y_TILES_IN_SBUF - 1)
+            if step < Y_TILES:
+                transpose_y(step)
+            if step >= MULTIPLY_LAG:
+                multiply_y(step - MULTIPLY_LAG)
+            if step - 1 < Y_TILES:
+                quantise_y(step - 1)
+            if step >= MULTIPLY_LAG:
+                empty_y(step - MULTIPLY_LAG)

@@ -66,7 +66,6 @@ def tile_causalselfattention_pc_t_kernel(tc, y_lat, W_uv, W_o, out):
             "planes": ctx.enter_context(tc.psum_pool(name="planes", bufs=4)),
         }
         acc_pool = ctx.enter_context(tc.psum_pool(name="acc", bufs=4))
-        ctx.enter_context(tc.manual_schedule())
 
         identity = keep.tile([P, P], F32)
         make_identity(nc, identity[:])

from contextlib import ExitStack

import concourse.mybir as mybir
from concourse.masks import make_identity

BF16 = mybir.dt.bfloat16
F32 = mybir.dt.float32
U32 = mybir.dt.uint32
U8 = mybir.dt.uint8
FP8X4 = mybir.dt.float8_e4m3fn_x4

P = 128
PACK = 4
K = P * PACK
WORDS = K // 2
HALVES = WORDS // P

B, NH, T, HS = 4, 4, 1024, 128
C = NH * HS
Y_TILES = B * NH
ROW_TILES = T // P
PAIR = 2
GROUPS_PER_BANK = 4

Y_TILES_IN_SBUF = 12
MULTIPLY_LAG = 2

FLOPS = 2 * K * K * C + 2 * B * NH * T * K * HS


def transpose_rows(nc, pools, identity, rows, row_tiles):
    row_words = rows.bitcast(F32)
    grouped = pools["grouped"].tile([P, row_tiles * P * PACK], BF16, tag="grouped", align_bytes=64)
    grouped_words = grouped[:].bitcast(F32)
    bank_words = PAIR * P * HALVES
    for pair in range(row_tiles // PAIR):
        planes = pools["planes"].tile([P, HALVES, PAIR * P], F32, tag="planes")
        for i in range(PAIR):
            for u in range(HALVES):
                word = (pair * PAIR + i) * WORDS + u * P
                nc.tensor.transpose(
                    planes[:, u, i * P : (i + 1) * P], row_words[:, word : word + P], identity
                )
        nc.scalar.copy(
            out=grouped_words[:, pair * bank_words : (pair + 1) * bank_words].rearrange(
                "p (n u) -> p n u", u=HALVES
            ),
            in_=planes[:].rearrange("p u n -> p n u"),
        )
    return grouped


def quantise(nc, grouped, codes, scales):
    nc.vector.quantize_mx(out=codes[:].bitcast(FP8X4), scales=scales[:], in_=grouped[:])


def tile_causalselfattention_pc_t_kernel(tc, y_lat, W_uv, W_o, out):
    nc = tc.nc
    with ExitStack() as ctx:
        keep = ctx.enter_context(tc.tile_pool(name="keep", bufs=1))
        y_pool = ctx.enter_context(tc.tile_pool(name="y_rows", bufs=Y_TILES_IN_SBUF))
        out_pool = ctx.enter_context(tc.tile_pool(name="result", bufs=B))
        mx_pool = ctx.enter_context(tc.tile_pool(name="mx", bufs=3))
        pools = {
            "grouped": ctx.enter_context(tc.tile_pool(name="grouped", bufs=3)),
            "planes": ctx.enter_context(tc.psum_pool(name="planes", bufs=4)),
        }
        acc_pool = ctx.enter_context(tc.psum_pool(name="acc", bufs=4))

        identity = keep.tile([P, P], F32)
        make_identity(nc, identity[:])

        uv_rows = keep.tile([P, PACK, K], BF16)
        nc.sync.dma_start(
            out=uv_rows[:].rearrange("p (u e) l -> p u e l", u=HALVES),
            in_=W_uv.rearrange("(u p e) l -> p u e l", u=HALVES, p=P),
        )
        wo_rows = keep.tile([P, NH * K], BF16)
        nc.sync.dma_start(
            out=wo_rows[:].rearrange("p (h j) -> p h j", h=NH),
            in_=W_o.rearrange("(h p) j -> p h j", p=P),
        )

        y_rows = {}

        def load_y(n):
            y_rows[n] = y_pool.tile([P, ROW_TILES * K], BF16, name="y_rows")
            nc.sync.dma_start(
                out=y_rows[n][:],
                in_=y_lat[n // NH, n % NH].rearrange("(p i) l -> p (i l)", i=ROW_TILES),
            )

        for n in range(Y_TILES_IN_SBUF):
            load_y(n)

        wo_grouped = transpose_rows(nc, pools, identity[:], wo_rows[:], NH)

        uv_grouped = pools["grouped"].tile([P, K * PACK], BF16, tag="grouped", align_bytes=64)
        uv_by_code = uv_rows[:].rearrange("p t (u m e) -> p t u m e", u=HALVES, m=P)
        for u in range(HALVES):
            for e in range(2):
                code = 2 * u + e
                nc.vector.tensor_copy(
                    out=uv_grouped[:, code * K : (code + 1) * K].rearrange("p (m t) -> p m t", t=PACK),
                    in_=uv_by_code[:, :, u, :, e].rearrange("p t m -> p m t"),
                )
        uv_codes = keep.tile([P, K], U32, align_bytes=64)
        uv_scales = keep.tile([P, K], U8, align_bytes=64)
        quantise(nc, uv_grouped, uv_codes, uv_scales)
        wo_codes = keep.tile([P, C], U32, align_bytes=64)
        wo_scales = keep.tile([P, C], U8, align_bytes=64)
        quantise(nc, wo_grouped, wo_codes, wo_scales)

        y_grouped, y_codes, y_scales, y_acc, results = {}, {}, {}, {}, {}
        v_codes = keep.tile([P, C], U32, align_bytes=64)
        v_scales = keep.tile([P, C], U8, align_bytes=64)

        def transpose_y(n):
            y_grouped[n] = transpose_rows(nc, pools, identity[:], y_rows[n][:], ROW_TILES)

        def quantise_y(n):
            y_codes[n] = mx_pool.tile([P, ROW_TILES * P], U32, name="y_codes", align_bytes=64)
            y_scales[n] = mx_pool.tile([P, ROW_TILES * P], U8, name="y_scales", align_bytes=64)
            quantise(nc, y_grouped[n], y_codes[n], y_scales[n])

        def multiply_y(n):
            head = slice((n % NH) * HS, (n % NH + 1) * HS)
            y_acc[n] = []
            for first in range(0, ROW_TILES, GROUPS_PER_BANK):
                acc = acc_pool.tile([P, GROUPS_PER_BANK, HS], F32, tag="acc")
                for g in range(GROUPS_PER_BANK):
                    tokens = slice((first + g) * P, (first + g + 1) * P)
                    nc.tensor.matmul_mx(
                        out=acc[:, g, :],
                        lhsT=y_codes[n][:, tokens].bitcast(FP8X4),
                        lhsT_scale=y_scales[n][:, tokens],
                        rhs=v_codes[:, head].bitcast(FP8X4),
                        rhs_scale=v_scales[:, head],
                        start=True,
                        stop=True,
                    )
                y_acc[n].append(acc)

        def empty_y(n):
            b, h = n // NH, n % NH
            if h == 0:
                results[b] = out_pool.tile([P, ROW_TILES, C], F32, name="result")
            out_rows = out[b].rearrange("(p i) c -> p i c", i=ROW_TILES)
            for bank, acc in enumerate(y_acc[n]):
                done = slice(bank * GROUPS_PER_BANK, (bank + 1) * GROUPS_PER_BANK)
                nc.vector.tensor_copy(out=results[b][:, done, h * HS : (h + 1) * HS], in_=acc[:])
                if h == NH - 1:
                    nc.sync.dma_start(out=out_rows[:, done, :], in_=results[b][:, done, :])

        transpose_y(0)

        v_grouped = pools["grouped"].tile([P, C * PACK], BF16, tag="grouped", align_bytes=64)
        for h in range(NH):
            head = slice(h * HS, (h + 1) * HS)
            v_acc = acc_pool.tile([P, PACK, HS], F32, tag="acc")
            for code in range(PACK):
                latent = slice(code * P, (code + 1) * P)
                nc.tensor.matmul_mx(
                    out=v_acc[:, code, :],
                    lhsT=uv_codes[:, latent].bitcast(FP8X4),
                    lhsT_scale=uv_scales[:, latent],
                    rhs=wo_codes[:, head].bitcast(FP8X4),
                    rhs_scale=wo_scales[:, head],
                    start=True,
                    stop=True,
                )
            nc.vector.tensor_copy(
                out=v_grouped[:, h * HS * PACK : (h + 1) * HS * PACK].rearrange("p (s t) -> p s t", t=PACK),
                in_=v_acc[:].rearrange("p t s -> p s t"),
            )
        quantise(nc, v_grouped, v_codes, v_scales)

        for step in range(1, Y_TILES + MULTIPLY_LAG):
            if step + Y_TILES_IN_SBUF - 1 < Y_TILES:
                load_y(step + Y_TILES_IN_SBUF - 1)
            if step < Y_TILES:
                transpose_y(step)
            if step >= MULTIPLY_LAG:
                multiply_y(step - MULTIPLY_LAG)
            if step - 1 < Y_TILES:
                quantise_y(step - 1)
            if step >= MULTIPLY_LAG:
                empty_y(step - MULTIPLY_LAG)
